import numpy as np
import ml_dtypes


def mxq(x, axis, fmt="e4m3"):
    dtype, down = {"e4m3": (ml_dtypes.float8_e4m3fn, 7), "e5m2": (ml_dtypes.float8_e5m2, 14)}[fmt]
    v = np.moveaxis(np.asarray(x, np.float32).astype(ml_dtypes.bfloat16).astype(np.float64), axis, -1)
    blocks = v.reshape(v.shape[:-1] + (-1, 32))
    amax = np.abs(blocks).max(-1, keepdims=True)
    byte = np.maximum(np.where(amax > 0, np.frexp(amax)[1] - 1 + 127, 0) - down, 1)
    scale = np.exp2(byte - 127.0)
    codes = (blocks / scale).astype(np.float32).astype(dtype).astype(np.float64)
    return np.moveaxis((codes * scale).reshape(v.shape), -1, axis)


WIDE = False


def mx_kscale(k):
    if not WIDE:
        return np.ones(k)
    levels = np.array([20, -20, 10, -10, 0])
    if k % 512:
        return np.exp2(np.random.permutation(np.resize(levels, k // 32))).repeat(32)
    a = np.empty((k // 512, 16))
    for p in range(k // 512):
        a[p, :8] = np.random.permutation(np.resize(levels, 8))
        for g in range(8):
            far = levels[np.abs(levels - a[p, g]) >= 10]
            a[p, g + 8] = far[np.random.randint(len(far))]
    return np.exp2(a.ravel()).repeat(32)


BF16 = ml_dtypes.bfloat16


def bf(x):
    return np.asarray(x, np.float32).astype(BF16)


def f64(x):
    return np.asarray(x).astype(np.float64)


B, L, F, A = 512, 12, 256, 512


def setup_inputs():
    u = mx_kscale(L * A).reshape(L, A)
    thresh = 1.0 / (A * L) ** 0.5
    inp = {"x": bf(np.random.standard_normal((B, L, F)))}
    for i in range(L):
        inp[f"W_{i}"] = bf(np.random.uniform(-thresh, thresh, (i + 1, F, A)) / u[i])
    g = np.random.standard_normal((B, L, A)) * np.exp2(np.random.randint(-12, 1, (B, 1, 1))) * 16.0 * u
    inp["grad_out"] = bf(g)
    return inp


def reference(x, W_0, W_1, W_2, W_3, W_4, W_5, W_6, W_7, W_8, W_9, W_10, W_11, grad_out):
    Ws = [W_0, W_1, W_2, W_3, W_4, W_5, W_6, W_7, W_8, W_9, W_10, W_11]
    gq = mxq(f64(grad_out).reshape(B, L * A), 1, "e5m2")
    Wq = [mxq(f64(Ws[i]).reshape((i + 1) * F, A), 1, "e4m3") for i in range(L)]
    gx = []
    for l in range(L):
        wl = np.concatenate([Wq[i][l * F : (l + 1) * F] for i in range(l, L)], axis=1)
        gx.append(gq[:, l * A :] @ wl.T)
    return np.stack(gx, axis=1)

@@ -1,0 +1,188 @@
+from contextlib import ExitStack
+
+import concourse.mybir as mybir
+from concourse.masks import make_identity
+
+BF16 = mybir.dt.bfloat16
+F32 = mybir.dt.float32
+I32 = mybir.dt.int32
+U32 = mybir.dt.uint32
+U8 = mybir.dt.uint8
+E4M3_X4 = mybir.dt.float8_e4m3fn_x4
+E5M2_X4 = mybir.dt.float8_e5m2_x4
+
+B, L, F, A = 512, 12, 256, 512
+P = 128
+PACK = 4
+SLAB_ROWS = 2 * P
+PANEL_ROWS = 2 * SLAB_ROWS
+PAIRS = L // 2
+B_TILES = B // P
+
+RAW_ROUNDS = 6
+
+LAYER_PAIRS = L * (L + 1) // 2
+FLOPS = 2 * B * F * A * LAYER_PAIRS
+BYTES = 2 * F * A * LAYER_PAIRS + 2 * B * L * A + 4 * B * L * F
+
+
+def turn_slab(nc, bank, words, identity):
+    for r in range(2):
+        for u in range(2):
+            nc.tensor.transpose(bank[:, 2 * r + u, :], words[:, r, u : 2 * P : 2], identity)
+
+
+def regroup(copy, grouped_slab, bank):
+    copy(
+        out=grouped_slab.bitcast(F32).rearrange("q (p c) -> q p c", c=4),
+        in_=bank.rearrange("q c p -> q p c"),
+    )
+
+
+def tile_decoder_pa_kernel(
+    tc, x, W_0, W_1, W_2, W_3, W_4, W_5, W_6, W_7, W_8, W_9, W_10, W_11, grad_out, out
+):
+    nc = tc.nc
+    weights = [W_0, W_1, W_2, W_3, W_4, W_5, W_6, W_7, W_8, W_9, W_10, W_11]
+
+    rounds = []
+    for j in reversed(range(PAIRS)):
+        for m in reversed(range(j, PAIRS)):
+            rounds.append(("weights", j, m))
+            if m == PAIRS - 1:
+                rounds.append(("gradients", j, j))
+
+    def slabs_in_panel(kind, j, i):
+        return 1 if kind == "weights" and i == 2 * j else 2
+
+    with ExitStack() as stack:
+        const = stack.enter_context(tc.tile_pool(name="const", bufs=1))
+        raw_pool = stack.enter_context(tc.tile_pool(name="raw", bufs=RAW_ROUNDS))
+        grouped_pool = stack.enter_context(tc.tile_pool(name="grouped", bufs=4))
+        weight_pool = stack.enter_context(tc.tile_pool(name="weight", bufs=6))
+        gradient_pool = stack.enter_context(tc.tile_pool(name="gradient", bufs=1))
+        result_pool = stack.enter_context(tc.tile_pool(name="result", bufs=2 * B_TILES))
+        turn_pool = stack.enter_context(tc.psum_pool(name="turn", bufs=4))
+        sum_pool = stack.enter_context(tc.psum_pool(name="sum", bufs=1))
+
+        identity = const.tile([P, P], F32, name="identity")
+        make_identity(nc, identity[:])
+
+        stack.enter_context(tc.manual_schedule())
+
+        raw_slabs = {}
+        gradient_operands = {}
+        sums = {}
+
+        def fetch(n):
+            kind, j, m = rounds[n]
+            raw = raw_pool.tile([P, 4, 2 * A], BF16, name="raw")
+            words = raw[:].bitcast(F32)
+            views = {}
+            for c in range(2):
+                if kind == "weights":
+                    i = 2 * m + c
+                    count = slabs_in_panel(kind, j, i)
+                    nc.sync.dma_start(
+                        out=raw[:, 2 * c : 2 * c + count, :],
+                        in_=weights[i][2 * j : 2 * j + count].rearrange("l (p r) a -> p l (r a)", r=2),
+                    )
+                    for h in range(count):
+                        views[(c, h)] = words[:, 2 * c + h, :].rearrange("p (r w) -> p r w", r=2)
+                else:
+                    nc.sync.dma_start(
+                        out=raw[:, 2 * c : 2 * c + 2, :],
+                        in_=grad_out[c * SLAB_ROWS : (c + 1) * SLAB_ROWS, 2 * m : 2 * m + 2, :].rearrange(
+                            "(p r) i a -> p r (i a)", r=2
+                        ),
+                    )
+                    for k in range(2):
+                        views[(k, c)] = words[:, 2 * c : 2 * c + 2, k * A // 2 : (k + 1) * A // 2]
+            raw_slabs[n] = views
+
+        def prepare(n):
+            kind, j, m = rounds[n]
+            slab_counts = [slabs_in_panel(kind, j, 2 * m + k) for k in range(2)]
+
+            banks = {}
+            for k in range(2):
+                for h in range(slab_counts[k]):
+                    bank = turn_pool.tile([P, 4, P], F32, name="bank")
+                    turn_slab(nc, bank, raw_slabs[n][(k, h)], identity[:])
+                    banks[(k, h)] = bank
+
+            grouped_tiles = []
+            for k in range(2):
+                grouped = grouped_pool.tile([P, PANEL_ROWS * PACK], BF16, name="grouped", align_bytes=64)
+                for h in range(slab_counts[k]):
+                    copy = nc.scalar.copy if h == 0 else nc.vector.tensor_copy
+                    columns = slice(h * SLAB_ROWS * PACK, (h + 1) * SLAB_ROWS * PACK)
+                    regroup(copy, grouped[:, columns], banks[(k, h)])
+                grouped_tiles.append(grouped)
+
+            operands = []
+            for k in range(2):
+                i = 2 * m + k
+                if kind == "gradients":
+                    codes = gradient_pool.tile([P, PANEL_ROWS], U32, name="g_codes%d" % i, align_bytes=64)
+                    scales = gradient_pool.tile([P, PANEL_ROWS], U8, name="g_scales%d" % i, align_bytes=64)
+                    packed = E5M2_X4
+                else:
+                    codes = weight_pool.tile([P, PANEL_ROWS], U32, name="w_codes", align_bytes=64)
+                    scales = weight_pool.tile([P, PANEL_ROWS], U8, name="w_scales", align_bytes=64)
+                    packed = E4M3_X4
+                rows = slab_counts[k] * SLAB_ROWS
+                if rows < PANEL_ROWS:
+                    nc.vector.memset(codes[:, rows:].bitcast(I32), 0)
+                    nc.vector.memset(scales[:, rows:].bitcast(I32), 0)
+                nc.vector.quantize_mx(
+                    out=codes[:, :rows].bitcast(packed),
+                    scales=scales[:, :rows],
+                    in_=grouped_tiles[k][:, : rows * PACK],
+                )
+                operands.append((codes, scales))
+                if kind == "gradients":
+                    gradient_operands[i] = (codes, scales)
+
+            if n + RAW_ROUNDS < len(rounds):
+                fetch(n + RAW_ROUNDS)
+            return operands
+
+        def multiply(j, m, weight_operands):
+            first, last = m == PAIRS - 1, m == j
+            for t in range(B_TILES):
+                if first:
+                    sums[t] = sum_pool.tile([P, PANEL_ROWS], F32, name="sum%d" % t)
+                b_columns = slice(t * P, (t + 1) * P)
+                for k in range(2):
+                    g_codes, g_scales = gradient_operands[2 * m + k]
+                    w_codes, w_scales = weight_operands[k]
+                    nc.tensor.matmul_mx(
+                        out=sums[t][:],
+                        lhsT=g_codes[:, b_columns].bitcast(E5M2_X4),
+                        lhsT_scale=g_scales[:, b_columns],
+                        rhs=w_codes[:].bitcast(E4M3_X4),
+                        rhs_scale=w_scales[:],
+                        start=(first and k == 0),
+                        stop=(last and k == 1),
+                    )
+            if last:
+                for t in range(B_TILES):
+                    result = result_pool.tile([P, PANEL_ROWS], F32, name="result")
+                    nc.scalar.copy(out=result[:], in_=sums[t][:])
+                    nc.sync.dma_start(
+                        out=out[t * P : (t + 1) * P, 2 * j : 2 * j + 2, :].rearrange("b l f -> b (l f)"),
+                        in_=result[:],
+                    )
+
+        for n in range(RAW_ROUNDS):
+            fetch(n)
+
+        waiting = None
+        for n, (kind, j, m) in enumerate(rounds):
+            operands = prepare(n)
+            if kind == "weights":
+                if waiting is not None:
+                    multiply(*waiting)
+                waiting = (j, m, operands)
+        multiply(*waiting)

@@ -26,10 +26,17 @@ FLOPS = 2 * B * F * A * LAYER_PAIRS
 BYTES = 2 * F * A * LAYER_PAIRS + 2 * B * L * A + 4 * B * L * F
 
 
+def reorder(nc, ordered, raw):
+    nc.vector.tensor_copy(
+        out=ordered.rearrange("p r (u g x) -> p r u g x", u=2, x=16),
+        in_=raw.rearrange("p r (g u x) -> p r u g x", u=2, x=16),
+    )
+
+
 def turn_slab(nc, bank, words, identity):
     for r in range(2):
         for u in range(2):
-            nc.tensor.transpose(bank[:, 2 * r + u, :], words[:, r, u : 2 * P : 2], identity)
+            nc.tensor.transpose(bank[:, 2 * r + u, :], words[:, r, u * P : (u + 1) * P], identity)
 
 
 def regroup(copy, grouped_slab, bank):
@@ -58,6 +65,7 @@ def tile_decoder_pa_kernel(
     with ExitStack() as stack:
         const = stack.enter_context(tc.tile_pool(name="const", bufs=1))
         raw_pool = stack.enter_context(tc.tile_pool(name="raw", bufs=RAW_ROUNDS))
+        ordered_pool = stack.enter_context(tc.tile_pool(name="ordered", bufs=3))
         grouped_pool = stack.enter_context(tc.tile_pool(name="grouped", bufs=4))
         weight_pool = stack.enter_context(tc.tile_pool(name="weight", bufs=6))
         gradient_pool = stack.enter_context(tc.tile_pool(name="gradient", bufs=1))
@@ -70,15 +78,14 @@ def tile_decoder_pa_kernel(
 
         stack.enter_context(tc.manual_schedule())
 
-        raw_slabs = {}
+        raw_rows = {}
+        ordered_slabs = {}
         gradient_operands = {}
         sums = {}
 
         def fetch(n):
             kind, j, m = rounds[n]
             raw = raw_pool.tile([P, 4, 2 * A], BF16, name="raw")
-            words = raw[:].bitcast(F32)
-            views = {}
             for c in range(2):
                 if kind == "weights":
                     i = 2 * m + c
@@ -87,8 +94,6 @@ def tile_decoder_pa_kernel(
                         out=raw[:, 2 * c : 2 * c + count, :],
                         in_=weights[i][2 * j : 2 * j + count].rearrange("l (p r) a -> p l (r a)", r=2),
                     )
-                    for h in range(count):
-                        views[(c, h)] = words[:, 2 * c + h, :].rearrange("p (r w) -> p r w", r=2)
                 else:
                     nc.sync.dma_start(
                         out=raw[:, 2 * c : 2 * c + 2, :],
@@ -96,28 +101,50 @@ def tile_decoder_pa_kernel(
                             "(p r) i a -> p r (i a)", r=2
                         ),
                     )
-                    for k in range(2):
-                        views[(k, c)] = words[:, 2 * c : 2 * c + 2, k * A // 2 : (k + 1) * A // 2]
-            raw_slabs[n] = views
+            raw_rows[n] = raw
+
+        def arrange(n):
+            kind, j, m = rounds[n]
+            raw = raw_rows[n]
+            ordered = ordered_pool.tile([P, 4, 2 * A], BF16, name="ordered")
+            words = ordered[:].bitcast(F32)
+            views = {}
+            for c in range(2):
+                count = slabs_in_panel(kind, j, 2 * m + c)
+                columns = slice(2 * c, 2 * c + count)
+                reorder(
+                    nc,
+                    ordered[:, columns, :].rearrange("p s (r a) -> p (s r) a", r=2),
+                    raw[:, columns, :].rearrange("p s (r a) -> p (s r) a", r=2),
+                )
+                for h in range(count):
+                    if kind == "weights":
+                        views[(c, h)] = words[:, 2 * c + h, :].rearrange("p (r w) -> p r w", r=2)
+                    else:
+                        views[(h, c)] = words[:, 2 * c : 2 * c + 2, h * A // 2 : (h + 1) * A // 2]
+            ordered_slabs[n] = views
+            if n + RAW_ROUNDS < len(rounds):
+                fetch(n + RAW_ROUNDS)
 
         def prepare(n):
             kind, j, m = rounds[n]
             slab_counts = [slabs_in_panel(kind, j, 2 * m + k) for k in range(2)]
+            if n + 2 < len(rounds):
+                arrange(n + 2)
 
             banks = {}
             for k in range(2):
                 for h in range(slab_counts[k]):
                     bank = turn_pool.tile([P, 4, P], F32, name="bank")
-                    turn_slab(nc, bank, raw_slabs[n][(k, h)], identity[:])
+                    turn_slab(nc, bank, ordered_slabs[n][(k, h)], identity[:])
                     banks[(k, h)] = bank
 
             grouped_tiles = []
             for k in range(2):
                 grouped = grouped_pool.tile([P, PANEL_ROWS * PACK], BF16, name="grouped", align_bytes=64)
                 for h in range(slab_counts[k]):
-                    copy = nc.scalar.copy if h == 0 else nc.vector.tensor_copy
                     columns = slice(h * SLAB_ROWS * PACK, (h + 1) * SLAB_ROWS * PACK)
-                    regroup(copy, grouped[:, columns], banks[(k, h)])
+                    regroup(nc.scalar.copy, grouped[:, columns], banks[(k, h)])
                 grouped_tiles.append(grouped)
 
             operands = []
@@ -144,8 +171,6 @@ def tile_decoder_pa_kernel(
                 if kind == "gradients":
                     gradient_operands[i] = (codes, scales)
 
-            if n + RAW_ROUNDS < len(rounds):
-                fetch(n + RAW_ROUNDS)
             return operands
 
         def multiply(j, m, weight_operands):
@@ -169,7 +194,8 @@ def tile_decoder_pa_kernel(
             if last:
                 for t in range(B_TILES):
                     result = result_pool.tile([P, PANEL_ROWS], F32, name="result")
-                    nc.scalar.copy(out=result[:], in_=sums[t][:])
+                    copy = nc.scalar.copy if t % 2 == 0 else nc.vector.tensor_copy
+                    copy(out=result[:], in_=sums[t][:])
                     nc.sync.dma_start(
                         out=out[t * P : (t + 1) * P, 2 * j : 2 * j + 2, :].rearrange("b l f -> b (l f)"),
                         in_=result[:],
@@ -177,6 +203,8 @@ def tile_decoder_pa_kernel(
 
         for n in range(RAW_ROUNDS):
             fetch(n)
+        for n in range(2):
+            arrange(n)
 
         waiting = None
         for n, (kind, j, m) in enumerate(rounds):

@@ -20,6 +20,8 @@ PAIRS = L // 2
 B_TILES = B // P
 
 RAW_ROUNDS = 6
+REORDER_AHEAD = 4
+LEAD = 2
 
 LAYER_PAIRS = L * (L + 1) // 2
 FLOPS = 2 * B * F * A * LAYER_PAIRS
@@ -53,11 +55,14 @@ def tile_decoder_pa_kernel(
     weights = [W_0, W_1, W_2, W_3, W_4, W_5, W_6, W_7, W_8, W_9, W_10, W_11]
 
     rounds = []
+    phase_end = {}
     for j in reversed(range(PAIRS)):
         for m in reversed(range(j, PAIRS)):
             rounds.append(("weights", j, m))
             if m == PAIRS - 1:
                 rounds.append(("gradients", j, j))
+        phase_end[j] = 2 * len(rounds)
+    panels = 2 * len(rounds)
 
     def slabs_in_panel(kind, j, i):
         return 1 if kind == "weights" and i == 2 * j else 2
@@ -65,13 +70,13 @@ def tile_decoder_pa_kernel(
     with ExitStack() as stack:
         const = stack.enter_context(tc.tile_pool(name="const", bufs=1))
         raw_pool = stack.enter_context(tc.tile_pool(name="raw", bufs=RAW_ROUNDS))
-        ordered_pool = stack.enter_context(tc.tile_pool(name="ordered", bufs=3))
+        ordered_pool = stack.enter_context(tc.tile_pool(name="ordered", bufs=4))
         grouped_pool = stack.enter_context(tc.tile_pool(name="grouped", bufs=4))
-        weight_pool = stack.enter_context(tc.tile_pool(name="weight", bufs=6))
+        weight_pool = stack.enter_context(tc.tile_pool(name="weight", bufs=4 * PAIRS - 2))
         gradient_pool = stack.enter_context(tc.tile_pool(name="gradient", bufs=1))
-        result_pool = stack.enter_context(tc.tile_pool(name="result", bufs=2 * B_TILES))
-        turn_pool = stack.enter_context(tc.psum_pool(name="turn", bufs=4))
-        sum_pool = stack.enter_context(tc.psum_pool(name="sum", bufs=1))
+        result_pool = stack.enter_context(tc.tile_pool(name="result", bufs=6))
+        turn_pool = stack.enter_context(tc.psum_pool(name="turn", bufs=6))
+        sum_pool = stack.enter_context(tc.psum_pool(name="sum", bufs=2))
 
         identity = const.tile([P, P], F32, name="identity")
         make_identity(nc, identity[:])
@@ -79,9 +84,10 @@ def tile_decoder_pa_kernel(
         stack.enter_context(tc.manual_schedule())
 
         raw_rows = {}
-        ordered_slabs = {}
+        ordered_rows = {}
+        grouped_panels = {}
+        weight_operands = {}
         gradient_operands = {}
-        sums = {}
 
         def fetch(n):
             kind, j, m = rounds[n]
@@ -103,114 +109,101 @@ def tile_decoder_pa_kernel(
                     )
             raw_rows[n] = raw
 
-        def arrange(n):
+        def arrange(half):
+            n, c = divmod(half, 2)
             kind, j, m = rounds[n]
-            raw = raw_rows[n]
-            ordered = ordered_pool.tile([P, 4, 2 * A], BF16, name="ordered")
-            words = ordered[:].bitcast(F32)
-            views = {}
-            for c in range(2):
-                count = slabs_in_panel(kind, j, 2 * m + c)
-                columns = slice(2 * c, 2 * c + count)
-                reorder(
-                    nc,
-                    ordered[:, columns, :].rearrange("p s (r a) -> p (s r) a", r=2),
-                    raw[:, columns, :].rearrange("p s (r a) -> p (s r) a", r=2),
-                )
-                for h in range(count):
-                    if kind == "weights":
-                        views[(c, h)] = words[:, 2 * c + h, :].rearrange("p (r w) -> p r w", r=2)
-                    else:
-                        views[(h, c)] = words[:, 2 * c : 2 * c + 2, h * A // 2 : (h + 1) * A // 2]
-            ordered_slabs[n] = views
-            if n + RAW_ROUNDS < len(rounds):
+            if c == 0:
+                ordered_rows[n] = ordered_pool.tile([P, 4, 2 * A], BF16, name="ordered")
+            columns = slice(2 * c, 2 * c + slabs_in_panel(kind, j, 2 * m + c))
+            reorder(
+                nc,
+                ordered_rows[n][:, columns, :].rearrange("p s (r a) -> p (s r) a", r=2),
+                raw_rows[n][:, columns, :].rearrange("p s (r a) -> p (s r) a", r=2),
+            )
+            if c == 1 and n + RAW_ROUNDS < len(rounds):
                 fetch(n + RAW_ROUNDS)
 
-        def prepare(n):
+        def turn(panel):
+            n, k = divmod(panel, 2)
             kind, j, m = rounds[n]
-            slab_counts = [slabs_in_panel(kind, j, 2 * m + k) for k in range(2)]
-            if n + 2 < len(rounds):
-                arrange(n + 2)
-
-            banks = {}
-            for k in range(2):
-                for h in range(slab_counts[k]):
-                    bank = turn_pool.tile([P, 4, P], F32, name="bank")
-                    turn_slab(nc, bank, ordered_slabs[n][(k, h)], identity[:])
-                    banks[(k, h)] = bank
-
-            grouped_tiles = []
-            for k in range(2):
-                grouped = grouped_pool.tile([P, PANEL_ROWS * PACK], BF16, name="grouped", align_bytes=64)
-                for h in range(slab_counts[k]):
-                    columns = slice(h * SLAB_ROWS * PACK, (h + 1) * SLAB_ROWS * PACK)
-                    regroup(nc.scalar.copy, grouped[:, columns], banks[(k, h)])
-                grouped_tiles.append(grouped)
-
-            operands = []
-            for k in range(2):
-                i = 2 * m + k
-                if kind == "gradients":
-                    codes = gradient_pool.tile([P, PANEL_ROWS], U32, name="g_codes%d" % i, align_bytes=64)
-                    scales = gradient_pool.tile([P, PANEL_ROWS], U8, name="g_scales%d" % i, align_bytes=64)
-                    packed = E5M2_X4
+            words = ordered_rows[n][:].bitcast(F32)
+            grouped = grouped_pool.tile([P, PANEL_ROWS * PACK], BF16, name="grouped", align_bytes=64)
+            for h in range(slabs_in_panel(kind, j, 2 * m + k)):
+                if kind == "weights":
+                    slab = words[:, 2 * k + h, :].rearrange("p (r w) -> p r w", r=2)
                 else:
-                    codes = weight_pool.tile([P, PANEL_ROWS], U32, name="w_codes", align_bytes=64)
-                    scales = weight_pool.tile([P, PANEL_ROWS], U8, name="w_scales", align_bytes=64)
-                    packed = E4M3_X4
-                rows = slab_counts[k] * SLAB_ROWS
-                if rows < PANEL_ROWS:
-                    nc.vector.memset(codes[:, rows:].bitcast(I32), 0)
-                    nc.vector.memset(scales[:, rows:].bitcast(I32), 0)
-                nc.vector.quantize_mx(
-                    out=codes[:, :rows].bitcast(packed),
-                    scales=scales[:, :rows],
-                    in_=grouped_tiles[k][:, : rows * PACK],
-                )
-                operands.append((codes, scales))
-                if kind == "gradients":
-                    gradient_operands[i] = (codes, scales)
+                    slab = words[:, 2 * h : 2 * h + 2, k * A // 2 : (k + 1) * A // 2]
+                bank = turn_pool.tile([P, 4, P], F32, name="bank")
+                turn_slab(nc, bank, slab, identity[:])
+                regroup(nc.scalar.copy, grouped[:, h * SLAB_ROWS * PACK : (h + 1) * SLAB_ROWS * PACK], bank)
+            grouped_panels[panel] = grouped
 
-            return operands
+        def quantise(panel):
+            n, k = divmod(panel, 2)
+            kind, j, m = rounds[n]
+            i = 2 * m + k
+            if kind == "gradients":
+                codes = gradient_pool.tile([P, PANEL_ROWS], U32, name="g_codes%d" % i, align_bytes=64)
+                scales = gradient_pool.tile([P, PANEL_ROWS], U8, name="g_scales%d" % i, align_bytes=64)
+                packed = E5M2_X4
+                gradient_operands[i] = (codes, scales)
+            else:
+                codes = weight_pool.tile([P, PANEL_ROWS], U32, name="w_codes", align_bytes=64)
+                scales = weight_pool.tile([P, PANEL_ROWS], U8, name="w_scales", align_bytes=64)
+                packed = E4M3_X4
+                weight_operands[(j, i)] = (codes, scales)
+            rows = slabs_in_panel(kind, j, i) * SLAB_ROWS
+            if rows < PANEL_ROWS:
+                nc.vector.memset(codes[:, rows:].bitcast(I32), 0)
+                nc.vector.memset(scales[:, rows:].bitcast(I32), 0)
+            nc.vector.quantize_mx(
+                out=codes[:, :rows].bitcast(packed),
+                scales=scales[:, :rows],
+                in_=grouped_panels[panel][:, : rows * PACK],
+            )
 
-        def multiply(j, m, weight_operands):
-            first, last = m == PAIRS - 1, m == j
-            for t in range(B_TILES):
-                if first:
-                    sums[t] = sum_pool.tile([P, PANEL_ROWS], F32, name="sum%d" % t)
+        def run(j, tiles):
+            layers = [i for m in reversed(range(j, PAIRS)) for i in (2 * m, 2 * m + 1)]
+            for t in tiles:
+                total = sum_pool.tile([P, PANEL_ROWS], F32, name="total")
                 b_columns = slice(t * P, (t + 1) * P)
-                for k in range(2):
-                    g_codes, g_scales = gradient_operands[2 * m + k]
-                    w_codes, w_scales = weight_operands[k]
+                for i in layers:
+                    g_codes, g_scales = gradient_operands[i]
+                    w_codes, w_scales = weight_operands[(j, i)]
                     nc.tensor.matmul_mx(
-                        out=sums[t][:],
+                        out=total[:],
                         lhsT=g_codes[:, b_columns].bitcast(E5M2_X4),
                         lhsT_scale=g_scales[:, b_columns],
                         rhs=w_codes[:].bitcast(E4M3_X4),
                         rhs_scale=w_scales[:],
-                        start=(first and k == 0),
-                        stop=(last and k == 1),
+                        start=(i == layers[0]),
+                        stop=(i == layers[-1]),
                     )
-            if last:
-                for t in range(B_TILES):
-                    result = result_pool.tile([P, PANEL_ROWS], F32, name="result")
-                    copy = nc.scalar.copy if t % 2 == 0 else nc.vector.tensor_copy
-                    copy(out=result[:], in_=sums[t][:])
-                    nc.sync.dma_start(
-                        out=out[t * P : (t + 1) * P, 2 * j : 2 * j + 2, :].rearrange("b l f -> b (l f)"),
-                        in_=result[:],
-                    )
+                result = result_pool.tile([P, PANEL_ROWS], F32, name="result")
+                nc.scalar.copy(out=result[:], in_=total[:])
+                nc.sync.dma_start(
+                    out=out[t * P : (t + 1) * P, 2 * j : 2 * j + 2, :].rearrange("b l f -> b (l f)"),
+                    in_=result[:],
+                )
 
         for n in range(RAW_ROUNDS):
             fetch(n)
-        for n in range(2):
-            arrange(n)
+        for half in range(REORDER_AHEAD):
+            arrange(half)
 
-        waiting = None
-        for n, (kind, j, m) in enumerate(rounds):
-            operands = prepare(n)
-            if kind == "weights":
-                if waiting is not None:
-                    multiply(*waiting)
-                waiting = (j, m, operands)
-        multiply(*waiting)
+        turned = 0
+        for j in reversed(range(PAIRS)):
+            tiles_per_run = 2 if j >= PAIRS // 2 else 1
+            ahead = phase_end[j - 1] - phase_end[j] if j > 0 else 0
+            for t in range(0, B_TILES, tiles_per_run):
+                goal = min(panels, phase_end[j] + LEAD + ahead * t // B_TILES)
+                while turned < goal:
+                    if turned + REORDER_AHEAD < panels:
+                        arrange(turned + REORDER_AHEAD)
+                    turn(turned)
+                    if turned > 0:
+                        quantise(turned - 1)
+                    turned += 1
+                    if turned == panels:
+                        quantise(turned - 1)
+                run(j, range(t, t + tiles_per_run))

@@ -41,9 +41,9 @@ def turn_slab(nc, bank, words, identity):
             nc.tensor.transpose(bank[:, 2 * r + u, :], words[:, r, u * P : (u + 1) * P], identity)
 
 
-def regroup(copy, grouped_slab, bank):
+def regroup(copy, target, bank):
     copy(
-        out=grouped_slab.bitcast(F32).rearrange("q (p c) -> q p c", c=4),
+        out=target,
         in_=bank.rearrange("q c p -> q p c"),
     )
 
@@ -97,8 +97,8 @@ def tile_decoder_pa_kernel(
                     i = 2 * m + c
                     count = slabs_in_panel(kind, j, i)
                     nc.sync.dma_start(
-                        out=raw[:, 2 * c : 2 * c + count, :],
-                        in_=weights[i][2 * j : 2 * j + count].rearrange("l (p r) a -> p l (r a)", r=2),
+                        out=raw[:, 2 * c : 2 * c + count, :].rearrange("p s x -> p (s x)"),
+                        in_=weights[i][2 * j : 2 * j + count].rearrange("l (p r) a -> (l p) (r a)", r=2 * count),
                     )
                 else:
                     nc.sync.dma_start(
@@ -135,7 +135,12 @@ def tile_decoder_pa_kernel(
                     slab = words[:, 2 * h : 2 * h + 2, k * A // 2 : (k + 1) * A // 2]
                 bank = turn_pool.tile([P, 4, P], F32, name="bank")
                 turn_slab(nc, bank, slab, identity[:])
-                regroup(nc.scalar.copy, grouped[:, h * SLAB_ROWS * PACK : (h + 1) * SLAB_ROWS * PACK], bank)
+                grouped_words = grouped[:].bitcast(F32)
+                if kind == "weights" and slabs_in_panel(kind, j, 2 * m + k) == 2:
+                    target = grouped_words.rearrange("q (p h c) -> q h p c", h=2, c=4)[:, h]
+                else:
+                    target = grouped_words.rearrange("q (h p c) -> q h p c", h=2, c=4)[:, h]
+                regroup(nc.scalar.copy, target, bank)
             grouped_panels[panel] = grouped
 
         def quantise(panel):

@@ -20,8 +20,8 @@ PAIRS = L // 2
 B_TILES = B // P
 
 RAW_ROUNDS = 6
-REORDER_AHEAD = 4
-LEAD = 2
+REORDER_AHEAD = 3
+LEAD = 3
 
 LAYER_PAIRS = L * (L + 1) // 2
 FLOPS = 2 * B * F * A * LAYER_PAIRS
@@ -72,7 +72,7 @@ def tile_decoder_pa_kernel(
         raw_pool = stack.enter_context(tc.tile_pool(name="raw", bufs=RAW_ROUNDS))
         ordered_pool = stack.enter_context(tc.tile_pool(name="ordered", bufs=4))
         grouped_pool = stack.enter_context(tc.tile_pool(name="grouped", bufs=4))
-        weight_pool = stack.enter_context(tc.tile_pool(name="weight", bufs=4 * PAIRS - 2))
+        weight_pool = stack.enter_context(tc.tile_pool(name="weight", bufs=4 * PAIRS - 4))
         gradient_pool = stack.enter_context(tc.tile_pool(name="gradient", bufs=1))
         result_pool = stack.enter_context(tc.tile_pool(name="result", bufs=6))
         turn_pool = stack.enter_context(tc.psum_pool(name="turn", bufs=6))
@@ -80,6 +80,14 @@ def tile_decoder_pa_kernel(
 
         identity = const.tile([P, P], F32, name="identity")
         make_identity(nc, identity[:])
+
+        half_operands = []
+        for e in range(2):
+            codes = const.tile([P, PANEL_ROWS], U32, name="half_codes%d" % e, align_bytes=64)
+            scales = const.tile([P, PANEL_ROWS], U8, name="half_scales%d" % e, align_bytes=64)
+            nc.gpsimd.memset(codes[:, SLAB_ROWS:].bitcast(I32), 0)
+            nc.gpsimd.memset(scales[:, SLAB_ROWS:].bitcast(I32), 0)
+            half_operands.append((codes, scales))
 
         stack.enter_context(tc.manual_schedule())
 
@@ -147,7 +155,11 @@ def tile_decoder_pa_kernel(
             n, k = divmod(panel, 2)
             kind, j, m = rounds[n]
             i = 2 * m + k
-            if kind == "gradients":
+            if slabs_in_panel(kind, j, i) == 1:
+                codes, scales = half_operands[j % 2]
+                packed = E4M3_X4
+                weight_operands[(j, i)] = (codes, scales)
+            elif kind == "gradients":
                 codes = gradient_pool.tile([P, PANEL_ROWS], U32, name="g_codes%d" % i, align_bytes=64)
                 scales = gradient_pool.tile([P, PANEL_ROWS], U8, name="g_scales%d" % i, align_bytes=64)
                 packed = E5M2_X4
@@ -158,9 +170,6 @@ def tile_decoder_pa_kernel(
                 packed = E4M3_X4
                 weight_operands[(j, i)] = (codes, scales)
             rows = slabs_in_panel(kind, j, i) * SLAB_ROWS
-            if rows < PANEL_ROWS:
-                nc.vector.memset(codes[:, rows:].bitcast(I32), 0)
-                nc.vector.memset(scales[:, rows:].bitcast(I32), 0)
             nc.vector.quantize_mx(
                 out=codes[:, :rows].bitcast(packed),
                 scales=scales[:, :rows],
@@ -205,9 +214,9 @@ def tile_decoder_pa_kernel(
                 while turned < goal:
                     if turned + REORDER_AHEAD < panels:
                         arrange(turned + REORDER_AHEAD)
-                    turn(turned)
                     if turned > 0:
                         quantise(turned - 1)
+                    turn(turned)
                     turned += 1
                     if turned == panels:
                         quantise(turned - 1)

@@ -20,8 +20,8 @@ PAIRS = L // 2
 B_TILES = B // P
 
 RAW_ROUNDS = 6
-REORDER_AHEAD = 3
-LEAD = 3
+REORDER_AHEAD = 4
+LEAD = 4
 
 LAYER_PAIRS = L * (L + 1) // 2
 FLOPS = 2 * B * F * A * LAYER_PAIRS
@@ -75,8 +75,7 @@ def tile_decoder_pa_kernel(
         weight_pool = stack.enter_context(tc.tile_pool(name="weight", bufs=4 * PAIRS - 4))
         gradient_pool = stack.enter_context(tc.tile_pool(name="gradient", bufs=1))
         result_pool = stack.enter_context(tc.tile_pool(name="result", bufs=6))
-        turn_pool = stack.enter_context(tc.psum_pool(name="turn", bufs=6))
-        sum_pool = stack.enter_context(tc.psum_pool(name="sum", bufs=2))
+        bank_pool = stack.enter_context(tc.psum_pool(name="banks", bufs=8))
 
         identity = const.tile([P, P], F32, name="identity")
         make_identity(nc, identity[:])
@@ -141,7 +140,7 @@ def tile_decoder_pa_kernel(
                     slab = words[:, 2 * k + h, :].rearrange("p (r w) -> p r w", r=2)
                 else:
                     slab = words[:, 2 * h : 2 * h + 2, k * A // 2 : (k + 1) * A // 2]
-                bank = turn_pool.tile([P, 4, P], F32, name="bank")
+                bank = bank_pool.tile([P, 4, P], F32, name="bank")
                 turn_slab(nc, bank, slab, identity[:])
                 grouped_words = grouped[:].bitcast(F32)
                 if kind == "weights" and slabs_in_panel(kind, j, 2 * m + k) == 2:
@@ -179,7 +178,7 @@ def tile_decoder_pa_kernel(
         def run(j, tiles):
             layers = [i for m in reversed(range(j, PAIRS)) for i in (2 * m, 2 * m + 1)]
             for t in tiles:
-                total = sum_pool.tile([P, PANEL_ROWS], F32, name="total")
+                total = bank_pool.tile([P, PANEL_ROWS], F32, name="bank")
                 b_columns = slice(t * P, (t + 1) * P)
                 for i in layers:
                     g_codes, g_scales = gradient_operands[i]
@@ -194,7 +193,8 @@ def tile_decoder_pa_kernel(
                         stop=(i == layers[-1]),
                     )
                 result = result_pool.tile([P, PANEL_ROWS], F32, name="result")
-                nc.scalar.copy(out=result[:], in_=total[:])
+                copy = nc.vector.tensor_copy if t == B_TILES - 1 else nc.scalar.copy
+                copy(out=result[:], in_=total[:])
                 nc.sync.dma_start(
                     out=out[t * P : (t + 1) * P, 2 * j : 2 * j + 2, :].rearrange("b l f -> b (l f)"),
                     in_=result[:],
@@ -207,7 +207,7 @@ def tile_decoder_pa_kernel(
 
         turned = 0
         for j in reversed(range(PAIRS)):
-            tiles_per_run = 2 if j >= PAIRS // 2 else 1
+            tiles_per_run = 2 if j > 0 else 1
             ahead = phase_end[j - 1] - phase_end[j] if j > 0 else 0
             for t in range(0, B_TILES, tiles_per_run):
                 goal = min(panels, phase_end[j] + LEAD + ahead * t // B_TILES)

from contextlib import ExitStack

import concourse.mybir as mybir
from concourse.masks import make_identity

BF16 = mybir.dt.bfloat16
F32 = mybir.dt.float32
I32 = mybir.dt.int32
U32 = mybir.dt.uint32
U8 = mybir.dt.uint8
E4M3_X4 = mybir.dt.float8_e4m3fn_x4
E5M2_X4 = mybir.dt.float8_e5m2_x4

B, L, F, A = 512, 12, 256, 512
P = 128
PACK = 4
SLAB_ROWS = 2 * P
PANEL_ROWS = 2 * SLAB_ROWS
PAIRS = L // 2
B_TILES = B // P

RAW_ROUNDS = 6
REORDER_AHEAD = 4
LEAD = 4

LAYER_PAIRS = L * (L + 1) // 2
FLOPS = 2 * B * F * A * LAYER_PAIRS
BYTES = 2 * F * A * LAYER_PAIRS + 2 * B * L * A + 4 * B * L * F


def reorder(nc, ordered, raw):
    nc.vector.tensor_copy(
        out=ordered.rearrange("p r (u g x) -> p r u g x", u=2, x=16),
        in_=raw.rearrange("p r (g u x) -> p r u g x", u=2, x=16),
    )


def turn_slab(nc, bank, words, identity):
    for r in range(2):
        for u in range(2):
            nc.tensor.transpose(bank[:, 2 * r + u, :], words[:, r, u * P : (u + 1) * P], identity)


def regroup(copy, target, bank):
    copy(
        out=target,
        in_=bank.rearrange("q c p -> q p c"),
    )


def tile_decoder_pa_kernel(
    tc, x, W_0, W_1, W_2, W_3, W_4, W_5, W_6, W_7, W_8, W_9, W_10, W_11, grad_out, out
):
    nc = tc.nc
    weights = [W_0, W_1, W_2, W_3, W_4, W_5, W_6, W_7, W_8, W_9, W_10, W_11]

    rounds = []
    phase_end = {}
    for j in reversed(range(PAIRS)):
        for m in reversed(range(j, PAIRS)):
            rounds.append(("weights", j, m))
            if m == PAIRS - 1:
                rounds.append(("gradients", j, j))
        phase_end[j] = 2 * len(rounds)
    panels = 2 * len(rounds)

    def slabs_in_panel(kind, j, i):
        return 1 if kind == "weights" and i == 2 * j else 2

    with ExitStack() as stack:
        const = stack.enter_context(tc.tile_pool(name="const", bufs=1))
        raw_pool = stack.enter_context(tc.tile_pool(name="raw", bufs=RAW_ROUNDS))
        ordered_pool = stack.enter_context(tc.tile_pool(name="ordered", bufs=4))
        grouped_pool = stack.enter_context(tc.tile_pool(name="grouped", bufs=4))
        weight_pool = stack.enter_context(tc.tile_pool(name="weight", bufs=4 * PAIRS - 4))
        gradient_pool = stack.enter_context(tc.tile_pool(name="gradient", bufs=1))
        result_pool = stack.enter_context(tc.tile_pool(name="result", bufs=6))
        bank_pool = stack.enter_context(tc.psum_pool(name="banks", bufs=8))

        identity = const.tile([P, P], F32, name="identity")
        make_identity(nc, identity[:])

        half_operands = []
        for e in range(2):
            codes = const.tile([P, PANEL_ROWS], U32, name="half_codes%d" % e, align_bytes=64)
            scales = const.tile([P, PANEL_ROWS], U8, name="half_scales%d" % e, align_bytes=64)
            nc.gpsimd.memset(codes[:, SLAB_ROWS:].bitcast(I32), 0)
            nc.gpsimd.memset(scales[:, SLAB_ROWS:].bitcast(I32), 0)
            half_operands.append((codes, scales))

        stack.enter_context(tc.manual_schedule())

        raw_rows = {}
        ordered_rows = {}
        grouped_panels = {}
        weight_operands = {}
        gradient_operands = {}

        def fetch(n):
            kind, j, m = rounds[n]
            raw = raw_pool.tile([P, 4, 2 * A], BF16, name="raw")
            for c in range(2):
                if kind == "weights":
                    i = 2 * m + c
                    count = slabs_in_panel(kind, j, i)
                    nc.sync.dma_start(
                        out=raw[:, 2 * c : 2 * c + count, :].rearrange("p s x -> p (s x)"),
                        in_=weights[i][2 * j : 2 * j + count].rearrange("l (p r) a -> (l p) (r a)", r=2 * count),
                    )
                else:
                    nc.sync.dma_start(
                        out=raw[:, 2 * c : 2 * c + 2, :],
                        in_=grad_out[c * SLAB_ROWS : (c + 1) * SLAB_ROWS, 2 * m : 2 * m + 2, :].rearrange(
                            "(p r) i a -> p r (i a)", r=2
                        ),
                    )
            raw_rows[n] = raw

        def arrange(half):
            n, c = divmod(half, 2)
            kind, j, m = rounds[n]
            if c == 0:
                ordered_rows[n] = ordered_pool.tile([P, 4, 2 * A], BF16, name="ordered")
            columns = slice(2 * c, 2 * c + slabs_in_panel(kind, j, 2 * m + c))
            reorder(
                nc,
                ordered_rows[n][:, columns, :].rearrange("p s (r a) -> p (s r) a", r=2),
                raw_rows[n][:, columns, :].rearrange("p s (r a) -> p (s r) a", r=2),
            )
            if c == 1 and n + RAW_ROUNDS < len(rounds):
                fetch(n + RAW_ROUNDS)

        def turn(panel):
            n, k = divmod(panel, 2)
            kind, j, m = rounds[n]
            words = ordered_rows[n][:].bitcast(F32)
            grouped = grouped_pool.tile([P, PANEL_ROWS * PACK], BF16, name="grouped", align_bytes=64)
            for h in range(slabs_in_panel(kind, j, 2 * m + k)):
                if kind == "weights":
                    slab = words[:, 2 * k + h, :].rearrange("p (r w) -> p r w", r=2)
                else:
                    slab = words[:, 2 * h : 2 * h + 2, k * A // 2 : (k + 1) * A // 2]
                bank = bank_pool.tile([P, 4, P], F32, name="bank")
                turn_slab(nc, bank, slab, identity[:])
                grouped_words = grouped[:].bitcast(F32)
                if kind == "weights" and slabs_in_panel(kind, j, 2 * m + k) == 2:
                    target = grouped_words.rearrange("q (p h c) -> q h p c", h=2, c=4)[:, h]
                else:
                    target = grouped_words.rearrange("q (h p c) -> q h p c", h=2, c=4)[:, h]
                regroup(nc.scalar.copy, target, bank)
            grouped_panels[panel] = grouped

        def quantise(panel):
            n, k = divmod(panel, 2)
            kind, j, m = rounds[n]
            i = 2 * m + k
            if slabs_in_panel(kind, j, i) == 1:
                codes, scales = half_operands[j % 2]
                packed = E4M3_X4
                weight_operands[(j, i)] = (codes, scales)
            elif kind == "gradients":
                codes = gradient_pool.tile([P, PANEL_ROWS], U32, name="g_codes%d" % i, align_bytes=64)
                scales = gradient_pool.tile([P, PANEL_ROWS], U8, name="g_scales%d" % i, align_bytes=64)
                packed = E5M2_X4
                gradient_operands[i] = (codes, scales)
            else:
                codes = weight_pool.tile([P, PANEL_ROWS], U32, name="w_codes", align_bytes=64)
                scales = weight_pool.tile([P, PANEL_ROWS], U8, name="w_scales", align_bytes=64)
                packed = E4M3_X4
                weight_operands[(j, i)] = (codes, scales)
            rows = slabs_in_panel(kind, j, i) * SLAB_ROWS
            nc.vector.quantize_mx(
                out=codes[:, :rows].bitcast(packed),
                scales=scales[:, :rows],
                in_=grouped_panels[panel][:, : rows * PACK],
            )

        def run(j, tiles):
            layers = [i for m in reversed(range(j, PAIRS)) for i in (2 * m, 2 * m + 1)]
            for t in tiles:
                total = bank_pool.tile([P, PANEL_ROWS], F32, name="bank")
                b_columns = slice(t * P, (t + 1) * P)
                for i in layers:
                    g_codes, g_scales = gradient_operands[i]
                    w_codes, w_scales = weight_operands[(j, i)]
                    nc.tensor.matmul_mx(
                        out=total[:],
                        lhsT=g_codes[:, b_columns].bitcast(E5M2_X4),
                        lhsT_scale=g_scales[:, b_columns],
                        rhs=w_codes[:].bitcast(E4M3_X4),
                        rhs_scale=w_scales[:],
                        start=(i == layers[0]),
                        stop=(i == layers[-1]),
                    )
                result = result_pool.tile([P, PANEL_ROWS], F32, name="result")
                copy = nc.vector.tensor_copy if t == B_TILES - 1 else nc.scalar.copy
                copy(out=result[:], in_=total[:])
                nc.sync.dma_start(
                    out=out[t * P : (t + 1) * P, 2 * j : 2 * j + 2, :].rearrange("b l f -> b (l f)"),
                    in_=result[:],
                )

        for n in range(RAW_ROUNDS):
            fetch(n)
        for half in range(REORDER_AHEAD):
            arrange(half)

        turned = 0
        for j in reversed(range(PAIRS)):
            tiles_per_run = 2 if j > 0 else 1
            ahead = phase_end[j - 1] - phase_end[j] if j > 0 else 0
            for t in range(0, B_TILES, tiles_per_run):
                goal = min(panels, phase_end[j] + LEAD + ahead * t // B_TILES)
                while turned < goal:
                    if turned + REORDER_AHEAD < panels:
                        arrange(turned + REORDER_AHEAD)
                    if turned > 0:
                        quantise(turned - 1)
                    turn(turned)
                    turned += 1
                    if turned == panels:
                        quantise(turned - 1)
                run(j, range(t, t + tiles_per_run))
